import numpy as np
import ml_dtypes


def mxq(x, axis, fmt="e4m3"):
    dtype, down = {"e4m3": (ml_dtypes.float8_e4m3fn, 7), "e5m2": (ml_dtypes.float8_e5m2, 14)}[fmt]
    v = np.moveaxis(np.asarray(x, np.float32).astype(ml_dtypes.bfloat16).astype(np.float64), axis, -1)
    blocks = v.reshape(v.shape[:-1] + (-1, 32))
    amax = np.abs(blocks).max(-1, keepdims=True)
    byte = np.maximum(np.where(amax > 0, np.frexp(amax)[1] - 1 + 127, 0) - down, 1)
    scale = np.exp2(byte - 127.0)
    codes = (blocks / scale).astype(np.float32).astype(dtype).astype(np.float64)
    return np.moveaxis((codes * scale).reshape(v.shape), -1, axis)


WIDE = False


def mx_kscale(k):
    if not WIDE:
        return np.ones(k)
    levels = np.array([10, -10, 5, -5, 0])
    a = np.random.permutation(np.resize(levels, k // 512 * 4)).reshape(k // 512, 4)
    idx = np.arange(k)
    return np.exp2(a[idx // 512, idx % 128 // 32])


BF16 = ml_dtypes.bfloat16


def bf(x):
    return np.asarray(x, np.float32).astype(BF16)


def f64(x):
    return np.asarray(x).astype(np.float64)


N, K, D_IN, HC, H = 4096, 4, 512, 512, 256


def sigmoid(v):
    return 1.0 / (1.0 + np.exp(-v))


def setup_inputs():
    s, t = mx_kscale(D_IN), mx_kscale(HC)
    d = {
        "x": bf(np.random.standard_normal((N, D_IN)) * s),
        "child_h": bf(np.random.standard_normal((N, K, HC)) * t),
        "fc_sum": bf(np.random.standard_normal((N, H)) * 0.27 * np.sqrt(K)),
    }
    for g in ("i", "o", "u"):
        d["W" + g] = bf(np.random.standard_normal((D_IN, H)) * 0.7 / np.sqrt(D_IN) / s[:, None])
        d["bW" + g] = bf(np.random.standard_normal(H) * 0.3)
        d["U" + g] = bf(np.random.standard_normal((HC, H)) * 0.7 / np.sqrt(K * HC) / t[:, None])
        d["bU" + g] = bf(np.random.standard_normal(H) * 0.3)
    return d


def reference(x, child_h, fc_sum, Wi, bWi, Ui, bUi, Wo, bWo, Uo, bUo, Wu, bWu, Uu, bUu):
    h_sum = f64(child_h).sum(axis=1)
    xq = mxq(f64(x), 1, "e4m3")
    hq = mxq(h_sum, 1, "e4m3")
    i = sigmoid((xq @ mxq(f64(Wi), 0, "e4m3")) + f64(bWi) + (hq @ mxq(f64(Ui), 0, "e4m3")) + f64(bUi))
    o = sigmoid((xq @ mxq(f64(Wo), 0, "e4m3")) + f64(bWo) + (hq @ mxq(f64(Uo), 0, "e4m3")) + f64(bUo))
    u = np.tanh((xq @ mxq(f64(Wu), 0, "e4m3")) + f64(bWu) + (hq @ mxq(f64(Uu), 0, "e4m3")) + f64(bUu))
    c = i * u + f64(fc_sum)
    h = o * np.tanh(c)
    return np.stack([h, c], axis=0)

@@ -1,0 +1,227 @@
+from contextlib import ExitStack
+
+import concourse.mybir as mybir
+from concourse.masks import make_identity
+
+F32 = mybir.dt.float32
+BF16 = mybir.dt.bfloat16
+U32 = mybir.dt.uint32
+U8 = mybir.dt.uint8
+FP8X4 = mybir.dt.float8_e4m3fn_x4
+ACT = mybir.ActivationFunctionType
+ALU = mybir.AluOpType
+
+P = 128
+PACK = 4
+NODES, CHILDREN, D, H = 4096, 4, 512, 256
+GATES = 3
+
+SLOTS = 4
+ROUND_NODES = P * SLOTS
+ROUNDS = NODES // ROUND_NODES
+GROUP_NODES = P // CHILDREN
+BANK_GROUPS = 4
+PG = GROUP_NODES // SLOTS
+PB = PG * BANK_GROUPS
+AHEAD = 2
+
+FLOPS = 2 * NODES * D * H * 2 * GATES
+
+
+def tile_childsumtreelstmcell_pb_t_kernel(
+    tc, x, child_h, fc_sum, Wi, bWi, Ui, bUi, Wo, bWo, Uo, bUo, Wu, bWu, Uu, bUu, out
+):
+    nc = tc.nc
+    with ExitStack() as ctx:
+        const = ctx.enter_context(tc.tile_pool(name="const", bufs=1))
+        loads = ctx.enter_context(tc.tile_pool(name="loads", bufs=AHEAD + 1))
+        grouped = ctx.enter_context(tc.tile_pool(name="grouped", bufs=2))
+        work = ctx.enter_context(tc.tile_pool(name="work", bufs=3))
+        psum_t = ctx.enter_context(tc.psum_pool(name="psum_t", bufs=1))
+        psum_g = ctx.enter_context(tc.psum_pool(name="psum_g", bufs=1))
+
+        x_view = x.rearrange("(r p j) d -> r p (j d)", p=P, j=SLOTS)
+        fc_view = fc_sum.rearrange("(r p j) d -> r p (j d)", p=P, j=SLOTS)
+        out_view = out.rearrange("o (r p j) d -> r p o (j d)", p=P, j=SLOTS)
+        ch_view = child_h.rearrange("n k d -> (n k) d").rearrange(
+            "(s g q) d -> s q g d", g=BANK_GROUPS, q=P
+        )
+
+        ident = const.tile([P, P], F32)
+        make_identity(nc, ident[:])
+        sel_nat = const.tile([P, GROUP_NODES], F32)
+        nc.vector.tensor_reduce(
+            out=sel_nat[:],
+            in_=ident[:].rearrange("q (n k) -> q n k", k=CHILDREN),
+            axis=mybir.AxisListType.X,
+            op=ALU.add,
+        )
+        sel = const.tile([P, SLOTS, PG], BF16)
+        nc.vector.tensor_copy(out=sel[:], in_=sel_nat[:].rearrange("q (a j) -> q j a", j=SLOTS))
+        warm = const.tile([P, 1], F32)
+        nc.vector.memset(warm[:], 0.0)
+        nc.scalar.activation(out=warm[:], in_=warm[:], func=ACT.Sigmoid)
+
+        def quantise_weights(mats, k_order, copy, name):
+            raw = const.tile([P, GATES, PACK, H], BF16, name=name + "_raw")
+            for g, mat in enumerate(mats):
+                k_order(raw[:, g], mat)
+            side = const.tile([P, GATES * H * PACK], BF16, align_bytes=64, name=name + "_side")
+            copy(
+                out=side[:].rearrange("w (g c t) -> w g c t", g=GATES, t=PACK),
+                in_=raw[:].rearrange("w g t c -> w g c t"),
+            )
+            codes = const.tile([P, GATES * H], U32, align_bytes=64, name=name + "_codes")
+            scales = const.tile([P, GATES * H], U8, align_bytes=64, name=name + "_scales")
+            for lo, hi in ((0, 2 * H), (2 * H, 3 * H)):
+                nc.vector.quantize_mx(
+                    out=codes[:, lo:hi].bitcast(FP8X4),
+                    scales=scales[:, lo:hi],
+                    in_=side[:, PACK * lo : PACK * hi],
+                )
+            return codes, scales
+
+        def load_w(dst, mat):
+            nc.sync.dma_start(
+                out=dst.rearrange("w (u e) c -> w u (e c)", u=2),
+                in_=mat.rearrange("(u w e) c -> w u (e c)", u=2, e=2),
+            )
+
+        def load_u(dst, mat):
+            nc.sync.dma_start(out=dst, in_=mat.rearrange("(t w) c -> w t c", w=P))
+
+        w_codes, w_scales = quantise_weights((Wi, Wo, Wu), load_w, nc.vector.tensor_copy, "w")
+        u_codes, u_scales = quantise_weights((Ui, Uo, Uu), load_u, nc.scalar.copy, "u")
+
+        bias_rows = const.tile([P, GATES * H], BF16)
+        nc.vector.memset(bias_rows[:], 0.0)
+        for g, (b_w, b_u) in enumerate(((bWi, bUi), (bWo, bUo), (bWu, bUu))):
+            cols = slice(H * g, H * (g + 1))
+            nc.gpsimd.dma_start(out=bias_rows[0:1, cols], in_=b_w.rearrange("(o h) -> o h", o=1))
+            nc.gpsimd.dma_start(out=bias_rows[1:2, cols], in_=b_u.rearrange("(o h) -> o h", o=1))
+        ones = const.tile([P, P], BF16)
+        nc.vector.memset(ones[:], 1.0)
+        bias = const.tile([P, GATES * H], F32)
+        bias_io_ps = psum_g.tile([P, 2 * H], F32, tag="io", bufs=3)
+        nc.tensor.matmul(
+            out=bias_io_ps[:], lhsT=ones[:], rhs=bias_rows[:, 0 : 2 * H], start=True, stop=True
+        )
+        nc.vector.tensor_copy(out=bias[:, 0 : 2 * H], in_=bias_io_ps[:])
+        bias_u_ps = psum_g.tile([P, 2, H], F32, tag="u", bufs=2)
+        nc.tensor.matmul(
+            out=bias_u_ps[:, 0, :], lhsT=ones[:], rhs=bias_rows[:, 2 * H : 3 * H], start=True, stop=True
+        )
+        nc.vector.tensor_copy(out=bias[:, 2 * H : 3 * H], in_=bias_u_ps[:, 0, :])
+
+        def load(r):
+            x_sb = loads.tile([P, SLOTS * D], BF16, tag="x")
+            nc.sync.dma_start(out=x_sb[:], in_=x_view[r])
+            fc_sb = loads.tile([P, SLOTS, H], BF16, tag="fc", bufs=AHEAD + 2)
+            nc.sync.dma_start(out=fc_sb[:].rearrange("p j d -> p (j d)"), in_=fc_view[r])
+            ch_sbs = []
+            for b in range(SLOTS):
+                ch_sb = loads.tile([P, BANK_GROUPS, D], BF16, tag="ch", bufs=SLOTS * (AHEAD + 1))
+                nc.sync.dma_start(out=ch_sb[:], in_=ch_view[SLOTS * r + b])
+                ch_sbs.append(ch_sb)
+            return x_sb, fc_sb, ch_sbs
+
+        def quantise_activations(x_sb, ch_sbs):
+            h_side = grouped.tile([P, SLOTS * P * PACK], BF16, align_bytes=64, tag="h_side")
+            h_side_v = h_side[:].rearrange("w (j p t) -> w j p t", j=SLOTS, t=PACK)
+            for b, ch_sb in enumerate(ch_sbs):
+                hT = psum_t.tile([P, SLOTS, PACK, PB], F32, tag="hT", bufs=2)
+                for g in range(BANK_GROUPS):
+                    for t in range(PACK):
+                        nc.tensor.matmul(
+                            out=hT[:, :, t, PG * g : PG * (g + 1)],
+                            lhsT=ch_sb[:, g, P * t : P * (t + 1)],
+                            rhs=sel[:],
+                            start=True,
+                            stop=True,
+                        )
+                nc.scalar.copy(
+                    out=h_side_v[:, :, PB * b : PB * (b + 1), :],
+                    in_=hT[:].rearrange("w j t p -> w j p t"),
+                )
+            x_side = grouped.tile([P, SLOTS * P * PACK], BF16, align_bytes=64, tag="x_side")
+            x_side_v = x_side[:].bitcast(F32).rearrange("w (j p u) -> w j p u", j=SLOTS, u=2)
+            x_words = x_sb[:].bitcast(F32)
+            for half in range(SLOTS // 2):
+                xT = psum_t.tile([P, 2, 2, P], F32, tag="xT", bufs=1)
+                for s in range(2):
+                    for u in range(2):
+                        first = (D // 2) * (2 * half + s) + P * u
+                        nc.tensor.transpose(xT[:, s, u, :], x_words[:, first : first + P], ident[:])
+                nc.vector.tensor_copy(
+                    out=x_side_v[:, 2 * half : 2 * half + 2, :, :],
+                    in_=xT[:].rearrange("w s u p -> w s p u"),
+                )
+            quantised = []
+            for side, name in ((x_side, "x"), (h_side, "h")):
+                codes = grouped.tile([P, SLOTS * P], U32, align_bytes=64, tag=name + "_codes", name=name + "_codes")
+                scales = grouped.tile([P, SLOTS * P], U8, align_bytes=64, tag=name + "_scales", name=name + "_scales")
+                nc.vector.quantize_mx(out=codes[:].bitcast(FP8X4), scales=scales[:], in_=side[:])
+                quantised.append((codes, scales))
+            return quantised
+
+        def gates_and_state(r, fc_sb, quantised):
+            (x_codes, x_scales), (h_codes, h_scales) = quantised
+            out_sb = work.tile([P, 2, SLOTS, H], F32, tag="out")
+            for half in range(SLOTS // 2):
+                pair = slice(2 * half, 2 * half + 2)
+                pre = work.tile([P, 2, GATES * H], F32, tag="pre")
+                u_ps = psum_g.tile([P, 2, H], F32, tag="u", bufs=2)
+                for s in range(2):
+                    nodes = slice(P * (2 * half + s), P * (2 * half + s + 1))
+                    io_ps = psum_g.tile([P, 2 * H], F32, tag="io", bufs=3)
+                    for acc, cols in ((io_ps[:], slice(0, 2 * H)), (u_ps[:, s, :], slice(2 * H, 3 * H))):
+                        nc.tensor.matmul_mx(
+                            out=acc,
+                            lhsT=x_codes[:, nodes].bitcast(FP8X4),
+                            lhsT_scale=x_scales[:, nodes],
+                            rhs=w_codes[:, cols].bitcast(FP8X4),
+                            rhs_scale=w_scales[:, cols],
+                            start=True,
+                            stop=False,
+                        )
+                        nc.tensor.matmul_mx(
+                            out=acc,
+                            lhsT=h_codes[:, nodes].bitcast(FP8X4),
+                            lhsT_scale=h_scales[:, nodes],
+                            rhs=u_codes[:, cols].bitcast(FP8X4),
+                            rhs_scale=u_scales[:, cols],
+                            start=False,
+                            stop=True,
+                        )
+                    nc.vector.tensor_tensor(
+                        out=pre[:, s, 0 : 2 * H], in0=io_ps[:], in1=bias[:, 0 : 2 * H], op=ALU.add
+                    )
+                nc.vector.tensor_tensor(
+                    out=pre[:, :, 2 * H : 3 * H],
+                    in0=u_ps[:],
+                    in1=bias[:, 2 * H : 3 * H].unsqueeze(1).to_broadcast([P, 2, H]),
+                    op=ALU.add,
+                )
+                nc.scalar.activation(out=pre[:, :, 0 : 2 * H], in_=pre[:, :, 0 : 2 * H], func=ACT.Sigmoid)
+                nc.scalar.activation(
+                    out=pre[:, :, 2 * H : 3 * H], in_=pre[:, :, 2 * H : 3 * H], func=ACT.Tanh
+                )
+                gate_i, gate_o, gate_u = pre[:, :, 0:H], pre[:, :, H : 2 * H], pre[:, :, 2 * H : 3 * H]
+                h_new, c_new = out_sb[:, 0, pair, :], out_sb[:, 1, pair, :]
+                nc.gpsimd.tensor_tensor(out=c_new, in0=gate_i, in1=gate_u, op=ALU.mult)
+                nc.gpsimd.tensor_tensor(out=c_new, in0=c_new, in1=fc_sb[:, pair, :], op=ALU.add)
+                tanh_c = work.tile([P, 2, H], F32, tag="tanh_c")
+                nc.scalar.activation(out=tanh_c[:], in_=c_new, func=ACT.Tanh)
+                nc.gpsimd.tensor_tensor(out=h_new, in0=gate_o, in1=tanh_c[:], op=ALU.mult)
+            nc.sync.dma_start(out=out_view[r], in_=out_sb[:].rearrange("p o j d -> p o (j d)"))
+
+        loaded = [load(r) for r in range(AHEAD)]
+        ready = []
+        for r in range(ROUNDS):
+            if r + AHEAD < ROUNDS:
+                loaded.append(load(r + AHEAD))
+            x_sb, fc_sb, ch_sbs = loaded[r]
+            ready.append(quantise_activations(x_sb, ch_sbs))
+            if r > 0:
+                gates_and_state(r - 1, loaded[r - 1][1], ready[r - 1])
+        gates_and_state(ROUNDS - 1, loaded[ROUNDS - 1][1], ready[ROUNDS - 1])

@@ -16,14 +16,14 @@ PACK = 4
 NODES, CHILDREN, D, H = 4096, 4, 512, 256
 GATES = 3
 
-SLOTS = 4
-ROUND_NODES = P * SLOTS
-ROUNDS = NODES // ROUND_NODES
+SLOTS = 2
+STEPS = NODES // (P * SLOTS)
 GROUP_NODES = P // CHILDREN
 BANK_GROUPS = 4
 PG = GROUP_NODES // SLOTS
 PB = PG * BANK_GROUPS
-AHEAD = 2
+LOAD_AHEAD = 4
+STORE_LAG = 2
 
 FLOPS = 2 * NODES * D * H * 2 * GATES
 
@@ -33,39 +33,36 @@ def tile_childsumtreelstmcell_pb_t_kernel(
 ):
     nc = tc.nc
     with ExitStack() as ctx:
+        ctx.enter_context(tc.manual_schedule())
         const = ctx.enter_context(tc.tile_pool(name="const", bufs=1))
-        loads = ctx.enter_context(tc.tile_pool(name="loads", bufs=AHEAD + 1))
-        grouped = ctx.enter_context(tc.tile_pool(name="grouped", bufs=2))
-        work = ctx.enter_context(tc.tile_pool(name="work", bufs=3))
-        psum_t = ctx.enter_context(tc.psum_pool(name="psum_t", bufs=1))
-        psum_g = ctx.enter_context(tc.psum_pool(name="psum_g", bufs=1))
+        loads = ctx.enter_context(tc.tile_pool(name="loads", bufs=LOAD_AHEAD))
+        sides = ctx.enter_context(tc.tile_pool(name="sides", bufs=2))
+        work = ctx.enter_context(tc.tile_pool(name="work", bufs=2))
+        psum = ctx.enter_context(tc.psum_pool(name="psum", bufs=1))
 
-        x_view = x.rearrange("(r p j) d -> r p (j d)", p=P, j=SLOTS)
-        fc_view = fc_sum.rearrange("(r p j) d -> r p (j d)", p=P, j=SLOTS)
-        out_view = out.rearrange("o (r p j) d -> r p o (j d)", p=P, j=SLOTS)
+        x_view = x.rearrange("(s p j) d -> s p (j d)", p=P, j=SLOTS)
+        fc_view = fc_sum.rearrange("(s p j) d -> s p (j d)", p=P, j=SLOTS)
+        out_view = out.rearrange("o (s p j) d -> s p o (j d)", p=P, j=SLOTS)
         ch_view = child_h.rearrange("n k d -> (n k) d").rearrange(
-            "(s g q) d -> s q g d", g=BANK_GROUPS, q=P
+            "(b g q) d -> b q g d", g=BANK_GROUPS, q=P
         )
 
-        ident = const.tile([P, P], F32)
-        make_identity(nc, ident[:])
-        sel_nat = const.tile([P, GROUP_NODES], F32)
-        nc.vector.tensor_reduce(
-            out=sel_nat[:],
-            in_=ident[:].rearrange("q (n k) -> q n k", k=CHILDREN),
-            axis=mybir.AxisListType.X,
-            op=ALU.add,
-        )
-        sel = const.tile([P, SLOTS, PG], BF16)
-        nc.vector.tensor_copy(out=sel[:], in_=sel_nat[:].rearrange("q (a j) -> q j a", j=SLOTS))
-        warm = const.tile([P, 1], F32)
-        nc.vector.memset(warm[:], 0.0)
-        nc.scalar.activation(out=warm[:], in_=warm[:], func=ACT.Sigmoid)
+        def load_w(dst, mat):
+            nc.sync.dma_start(
+                out=dst.rearrange("w (u e) c -> w u (e c)", u=2),
+                in_=mat.rearrange("(u w e) c -> w u (e c)", u=2, e=2),
+            )
 
-        def quantise_weights(mats, k_order, copy, name):
+        def load_u(dst, mat):
+            nc.sync.dma_start(out=dst, in_=mat.rearrange("(t w) c -> w t c", w=P))
+
+        def load_weights(mats, k_order, name):
             raw = const.tile([P, GATES, PACK, H], BF16, name=name + "_raw")
             for g, mat in enumerate(mats):
                 k_order(raw[:, g], mat)
+            return raw
+
+        def quantise_weights(raw, copy, name):
             side = const.tile([P, GATES * H * PACK], BF16, align_bytes=64, name=name + "_side")
             copy(
                 out=side[:].rearrange("w (g c t) -> w g c t", g=GATES, t=PACK),
@@ -81,18 +78,11 @@ def tile_childsumtreelstmcell_pb_t_kernel(
                 )
             return codes, scales
 
-        def load_w(dst, mat):
-            nc.sync.dma_start(
-                out=dst.rearrange("w (u e) c -> w u (e c)", u=2),
-                in_=mat.rearrange("(u w e) c -> w u (e c)", u=2, e=2),
-            )
+        u_raw = load_weights((Ui, Uo, Uu), load_u, "u")
+        w_raw = load_weights((Wi, Wo, Wu), load_w, "w")
 
-        def load_u(dst, mat):
-            nc.sync.dma_start(out=dst, in_=mat.rearrange("(t w) c -> w t c", w=P))
-
-        w_codes, w_scales = quantise_weights((Wi, Wo, Wu), load_w, nc.vector.tensor_copy, "w")
-        u_codes, u_scales = quantise_weights((Ui, Uo, Uu), load_u, nc.scalar.copy, "u")
-
+        ident = const.tile([P, P], F32)
+        make_identity(nc, ident[:])
         bias_rows = const.tile([P, GATES * H], BF16)
         nc.vector.memset(bias_rows[:], 0.0)
         for g, (b_w, b_u) in enumerate(((bWi, bUi), (bWo, bUo), (bWu, bUu))):
@@ -101,127 +91,204 @@ def tile_childsumtreelstmcell_pb_t_kernel(
             nc.gpsimd.dma_start(out=bias_rows[1:2, cols], in_=b_u.rearrange("(o h) -> o h", o=1))
         ones = const.tile([P, P], BF16)
         nc.vector.memset(ones[:], 1.0)
+        warm = const.tile([P, 1], F32)
+        nc.vector.memset(warm[:], 0.0)
+        nc.scalar.activation(out=warm[:], in_=warm[:], func=ACT.Sigmoid)
+        sel_nat = const.tile([P, GROUP_NODES], F32)
+        nc.vector.tensor_reduce(
+            out=sel_nat[:],
+            in_=ident[:].rearrange("q (n k) -> q n k", k=CHILDREN),
+            axis=mybir.AxisListType.X,
+            op=ALU.add,
+        )
+        sel = const.tile([P, SLOTS, PG], BF16)
+        nc.vector.tensor_copy(out=sel[:], in_=sel_nat[:].rearrange("q (a j) -> q j a", j=SLOTS))
+
+        w_codes, w_scales = quantise_weights(w_raw, nc.vector.tensor_copy, "w")
+        u_codes, u_scales = quantise_weights(u_raw, nc.scalar.copy, "u")
         bias = const.tile([P, GATES * H], F32)
-        bias_io_ps = psum_g.tile([P, 2 * H], F32, tag="io", bufs=3)
-        nc.tensor.matmul(
-            out=bias_io_ps[:], lhsT=ones[:], rhs=bias_rows[:, 0 : 2 * H], start=True, stop=True
-        )
-        nc.vector.tensor_copy(out=bias[:, 0 : 2 * H], in_=bias_io_ps[:])
-        bias_u_ps = psum_g.tile([P, 2, H], F32, tag="u", bufs=2)
-        nc.tensor.matmul(
-            out=bias_u_ps[:, 0, :], lhsT=ones[:], rhs=bias_rows[:, 2 * H : 3 * H], start=True, stop=True
-        )
-        nc.vector.tensor_copy(out=bias[:, 2 * H : 3 * H], in_=bias_u_ps[:, 0, :])
 
-        def load(r):
-            x_sb = loads.tile([P, SLOTS * D], BF16, tag="x")
-            nc.sync.dma_start(out=x_sb[:], in_=x_view[r])
-            fc_sb = loads.tile([P, SLOTS, H], BF16, tag="fc", bufs=AHEAD + 2)
-            nc.sync.dma_start(out=fc_sb[:].rearrange("p j d -> p (j d)"), in_=fc_view[r])
-            ch_sbs = []
+        def build_bias():
+            bias_io_ps = psum.tile([P, 2 * H], F32, tag="io", bufs=3)
+            nc.tensor.matmul(
+                out=bias_io_ps[:], lhsT=ones[:], rhs=bias_rows[:, 0 : 2 * H], start=True, stop=True
+            )
+            nc.vector.tensor_copy(out=bias[:, 0 : 2 * H], in_=bias_io_ps[:])
+            bias_u_ps = psum.tile([P, SLOTS, H], F32, tag="u", bufs=2)
+            nc.tensor.matmul(
+                out=bias_u_ps[:, 0, :],
+                lhsT=ones[:],
+                rhs=bias_rows[:, 2 * H : 3 * H],
+                start=True,
+                stop=True,
+            )
+            nc.vector.tensor_copy(out=bias[:, 2 * H : 3 * H], in_=bias_u_ps[:, 0, :])
+
+        x_sb, fc_sb, ch_sb, hT_ps, xT_ps = {}, {}, {}, {}, {}
+        x_side, h_side, x_q, h_q, io_ps, u_ps = {}, {}, {}, {}, {}, {}
+        pre, tanh_c, out_sb = {}, {}, {}
+
+        def live(s):
+            return 0 <= s < STEPS
+
+        def load(s):
+            if not live(s):
+                return
+            x_sb[s] = loads.tile([P, SLOTS * D], BF16, tag="x", name="x_sb")
+            nc.sync.dma_start(out=x_sb[s][:], in_=x_view[s])
             for b in range(SLOTS):
-                ch_sb = loads.tile([P, BANK_GROUPS, D], BF16, tag="ch", bufs=SLOTS * (AHEAD + 1))
-                nc.sync.dma_start(out=ch_sb[:], in_=ch_view[SLOTS * r + b])
-                ch_sbs.append(ch_sb)
-            return x_sb, fc_sb, ch_sbs
+                ch_sb[s, b] = loads.tile(
+                    [P, BANK_GROUPS, D], BF16, tag="ch", bufs=SLOTS * (LOAD_AHEAD + 1), name="ch_sb"
+                )
+                nc.sync.dma_start(out=ch_sb[s, b][:], in_=ch_view[SLOTS * s + b])
+            fc_sb[s] = loads.tile([P, SLOTS, H], BF16, tag="fc", bufs=LOAD_AHEAD + 3, name="fc_sb")
+            nc.sync.dma_start(out=fc_sb[s][:].rearrange("p j d -> p (j d)"), in_=fc_view[s])
 
-        def quantise_activations(x_sb, ch_sbs):
-            h_side = grouped.tile([P, SLOTS * P * PACK], BF16, align_bytes=64, tag="h_side")
-            h_side_v = h_side[:].rearrange("w (j p t) -> w j p t", j=SLOTS, t=PACK)
-            for b, ch_sb in enumerate(ch_sbs):
-                hT = psum_t.tile([P, SLOTS, PACK, PB], F32, tag="hT", bufs=2)
+        def sum_children(s):
+            if not live(s):
+                return
+            for b in range(SLOTS):
+                hT_ps[s, b] = psum.tile([P, SLOTS, PACK, PB], F32, tag="hT", bufs=2, name="hT_ps")
                 for g in range(BANK_GROUPS):
                     for t in range(PACK):
                         nc.tensor.matmul(
-                            out=hT[:, :, t, PG * g : PG * (g + 1)],
-                            lhsT=ch_sb[:, g, P * t : P * (t + 1)],
+                            out=hT_ps[s, b][:, :, t, PG * g : PG * (g + 1)],
+                            lhsT=ch_sb[s, b][:, g, P * t : P * (t + 1)],
                             rhs=sel[:],
                             start=True,
                             stop=True,
                         )
+
+        def round_h(s):
+            if not live(s):
+                return
+            h_side[s] = sides.tile([P, SLOTS * P * PACK], BF16, align_bytes=64, tag="h_side", name="h_side")
+            view = h_side[s][:].rearrange("w (j p t) -> w j p t", j=SLOTS, t=PACK)
+            for b in range(SLOTS):
                 nc.scalar.copy(
-                    out=h_side_v[:, :, PB * b : PB * (b + 1), :],
-                    in_=hT[:].rearrange("w j t p -> w j p t"),
+                    out=view[:, :, PB * b : PB * (b + 1), :],
+                    in_=hT_ps[s, b][:].rearrange("w j t p -> w j p t"),
                 )
-            x_side = grouped.tile([P, SLOTS * P * PACK], BF16, align_bytes=64, tag="x_side")
-            x_side_v = x_side[:].bitcast(F32).rearrange("w (j p u) -> w j p u", j=SLOTS, u=2)
-            x_words = x_sb[:].bitcast(F32)
-            for half in range(SLOTS // 2):
-                xT = psum_t.tile([P, 2, 2, P], F32, tag="xT", bufs=1)
-                for s in range(2):
-                    for u in range(2):
-                        first = (D // 2) * (2 * half + s) + P * u
-                        nc.tensor.transpose(xT[:, s, u, :], x_words[:, first : first + P], ident[:])
-                nc.vector.tensor_copy(
-                    out=x_side_v[:, 2 * half : 2 * half + 2, :, :],
-                    in_=xT[:].rearrange("w s u p -> w s p u"),
-                )
-            quantised = []
-            for side, name in ((x_side, "x"), (h_side, "h")):
-                codes = grouped.tile([P, SLOTS * P], U32, align_bytes=64, tag=name + "_codes", name=name + "_codes")
-                scales = grouped.tile([P, SLOTS * P], U8, align_bytes=64, tag=name + "_scales", name=name + "_scales")
-                nc.vector.quantize_mx(out=codes[:].bitcast(FP8X4), scales=scales[:], in_=side[:])
-                quantised.append((codes, scales))
-            return quantised
 
-        def gates_and_state(r, fc_sb, quantised):
-            (x_codes, x_scales), (h_codes, h_scales) = quantised
-            out_sb = work.tile([P, 2, SLOTS, H], F32, tag="out")
-            for half in range(SLOTS // 2):
-                pair = slice(2 * half, 2 * half + 2)
-                pre = work.tile([P, 2, GATES * H], F32, tag="pre")
-                u_ps = psum_g.tile([P, 2, H], F32, tag="u", bufs=2)
-                for s in range(2):
-                    nodes = slice(P * (2 * half + s), P * (2 * half + s + 1))
-                    io_ps = psum_g.tile([P, 2 * H], F32, tag="io", bufs=3)
-                    for acc, cols in ((io_ps[:], slice(0, 2 * H)), (u_ps[:, s, :], slice(2 * H, 3 * H))):
+        def transpose_x(s):
+            if not live(s):
+                return
+            xT_ps[s] = psum.tile([P, SLOTS, 2, P], F32, tag="xT", bufs=1, name="xT_ps")
+            words = x_sb[s][:].bitcast(F32)
+            for j in range(SLOTS):
+                for u in range(2):
+                    first = (D // 2) * j + P * u
+                    nc.tensor.transpose(xT_ps[s][:, j, u, :], words[:, first : first + P], ident[:])
+
+        def copy_x(s):
+            if not live(s):
+                return
+            x_side[s] = sides.tile([P, SLOTS * P * PACK], BF16, align_bytes=64, tag="x_side", name="x_side")
+            nc.vector.tensor_copy(
+                out=x_side[s][:].bitcast(F32).rearrange("w (j p u) -> w j p u", j=SLOTS, u=2),
+                in_=xT_ps[s][:].rearrange("w j u p -> w j p u"),
+            )
+
+        def quantise(s, side, quantised, name):
+            if not live(s):
+                return
+            codes = sides.tile([P, SLOTS * P], U32, align_bytes=64, tag=name + "_codes", name=name + "_codes")
+            scales = sides.tile([P, SLOTS * P], U8, align_bytes=64, tag=name + "_scales", name=name + "_scales")
+            nc.vector.quantize_mx(out=codes[:].bitcast(FP8X4), scales=scales[:], in_=side[s][:])
+            quantised[s] = (codes, scales)
+
+        def multiply(s):
+            if not live(s):
+                return
+            u_ps[s] = psum.tile([P, SLOTS, H], F32, tag="u", bufs=2, name="u_ps")
+            for j in range(SLOTS):
+                nodes = slice(P * j, P * (j + 1))
+                io_ps[s, j] = psum.tile([P, 2 * H], F32, tag="io", bufs=3, name="io_ps")
+                for acc, cols in (
+                    (io_ps[s, j][:], slice(0, 2 * H)),
+                    (u_ps[s][:, j, :], slice(2 * H, 3 * H)),
+                ):
+                    for part, (a_q, b_codes, b_scales) in enumerate(
+                        ((x_q[s], w_codes, w_scales), (h_q[s], u_codes, u_scales))
+                    ):
                         nc.tensor.matmul_mx(
                             out=acc,
-                            lhsT=x_codes[:, nodes].bitcast(FP8X4),
-                            lhsT_scale=x_scales[:, nodes],
-                            rhs=w_codes[:, cols].bitcast(FP8X4),
-                            rhs_scale=w_scales[:, cols],
-                            start=True,
-                            stop=False,
+                            lhsT=a_q[0][:, nodes].bitcast(FP8X4),
+                            lhsT_scale=a_q[1][:, nodes],
+                            rhs=b_codes[:, cols].bitcast(FP8X4),
+                            rhs_scale=b_scales[:, cols],
+                            start=(part == 0),
+                            stop=(part == 1),
                         )
-                        nc.tensor.matmul_mx(
-                            out=acc,
-                            lhsT=h_codes[:, nodes].bitcast(FP8X4),
-                            lhsT_scale=h_scales[:, nodes],
-                            rhs=u_codes[:, cols].bitcast(FP8X4),
-                            rhs_scale=u_scales[:, cols],
-                            start=False,
-                            stop=True,
-                        )
-                    nc.vector.tensor_tensor(
-                        out=pre[:, s, 0 : 2 * H], in0=io_ps[:], in1=bias[:, 0 : 2 * H], op=ALU.add
-                    )
+
+        def add_bias(s):
+            if not live(s):
+                return
+            pre[s] = work.tile([P, SLOTS, GATES * H], F32, tag="pre", bufs=4, name="pre")
+            for j in range(SLOTS):
                 nc.vector.tensor_tensor(
-                    out=pre[:, :, 2 * H : 3 * H],
-                    in0=u_ps[:],
-                    in1=bias[:, 2 * H : 3 * H].unsqueeze(1).to_broadcast([P, 2, H]),
-                    op=ALU.add,
+                    out=pre[s][:, j, 0 : 2 * H], in0=io_ps[s, j][:], in1=bias[:, 0 : 2 * H], op=ALU.add
                 )
-                nc.scalar.activation(out=pre[:, :, 0 : 2 * H], in_=pre[:, :, 0 : 2 * H], func=ACT.Sigmoid)
-                nc.scalar.activation(
-                    out=pre[:, :, 2 * H : 3 * H], in_=pre[:, :, 2 * H : 3 * H], func=ACT.Tanh
-                )
-                gate_i, gate_o, gate_u = pre[:, :, 0:H], pre[:, :, H : 2 * H], pre[:, :, 2 * H : 3 * H]
-                h_new, c_new = out_sb[:, 0, pair, :], out_sb[:, 1, pair, :]
-                nc.gpsimd.tensor_tensor(out=c_new, in0=gate_i, in1=gate_u, op=ALU.mult)
-                nc.gpsimd.tensor_tensor(out=c_new, in0=c_new, in1=fc_sb[:, pair, :], op=ALU.add)
-                tanh_c = work.tile([P, 2, H], F32, tag="tanh_c")
-                nc.scalar.activation(out=tanh_c[:], in_=c_new, func=ACT.Tanh)
-                nc.gpsimd.tensor_tensor(out=h_new, in0=gate_o, in1=tanh_c[:], op=ALU.mult)
-            nc.sync.dma_start(out=out_view[r], in_=out_sb[:].rearrange("p o j d -> p o (j d)"))
+            nc.vector.tensor_tensor(
+                out=pre[s][:, :, 2 * H : 3 * H],
+                in0=u_ps[s][:],
+                in1=bias[:, 2 * H : 3 * H].unsqueeze(1).to_broadcast([P, SLOTS, H]),
+                op=ALU.add,
+            )
 
-        loaded = [load(r) for r in range(AHEAD)]
-        ready = []
-        for r in range(ROUNDS):
-            if r + AHEAD < ROUNDS:
-                loaded.append(load(r + AHEAD))
-            x_sb, fc_sb, ch_sbs = loaded[r]
-            ready.append(quantise_activations(x_sb, ch_sbs))
-            if r > 0:
-                gates_and_state(r - 1, loaded[r - 1][1], ready[r - 1])
-        gates_and_state(ROUNDS - 1, loaded[ROUNDS - 1][1], ready[ROUNDS - 1])
+        def activate(s):
+            if not live(s):
+                return
+            gates_io, gate_u = pre[s][:, :, 0 : 2 * H], pre[s][:, :, 2 * H : 3 * H]
+            nc.scalar.activation(out=gates_io, in_=gates_io, func=ACT.Sigmoid)
+            nc.scalar.activation(out=gate_u, in_=gate_u, func=ACT.Tanh)
+
+        def cell(s):
+            if not live(s):
+                return
+            out_sb[s] = work.tile([P, 2, SLOTS, H], F32, tag="out", bufs=STORE_LAG + 4, name="out_sb")
+            c_new = out_sb[s][:, 1]
+            nc.gpsimd.tensor_tensor(
+                out=c_new, in0=pre[s][:, :, 0:H], in1=pre[s][:, :, 2 * H : 3 * H], op=ALU.mult
+            )
+            nc.gpsimd.tensor_tensor(out=c_new, in0=c_new, in1=fc_sb[s][:], op=ALU.add)
+
+        def tanh_cell(s):
+            if not live(s):
+                return
+            tanh_c[s] = work.tile([P, SLOTS, H], F32, tag="tanh_c", name="tanh_c")
+            nc.scalar.activation(out=tanh_c[s][:], in_=out_sb[s][:, 1], func=ACT.Tanh)
+
+        def hidden(s):
+            if not live(s):
+                return
+            nc.vector.tensor_tensor(
+                out=out_sb[s][:, 0], in0=pre[s][:, :, H : 2 * H], in1=tanh_c[s][:], op=ALU.mult
+            )
+
+        def store(s):
+            if not live(s):
+                return
+            nc.sync.dma_start(out=out_view[s], in_=out_sb[s][:].rearrange("p o j d -> p o (j d)"))
+
+        def iteration(t):
+            load(t + LOAD_AHEAD)
+            store(t - 3 - STORE_LAG)
+            sum_children(t + 1)
+            copy_x(t + 1)
+            hidden(t - 3)
+            quantise(t + 1, x_side, x_q, "x")
+            activate(t - 1)
+            cell(t - 1)
+            round_h(t + 1)
+            multiply(t)
+            add_bias(t)
+            quantise(t + 1, h_side, h_q, "h")
+            tanh_cell(t - 2)
+            transpose_x(t + 2)
+
+        for t in range(-LOAD_AHEAD, 0):
+            iteration(t)
+        build_bias()
+        for t in range(0, STEPS + 3 + STORE_LAG + 1):
+            iteration(t)

@@ -22,8 +22,8 @@ GROUP_NODES = P // CHILDREN
 BANK_GROUPS = 4
 PG = GROUP_NODES // SLOTS
 PB = PG * BANK_GROUPS
-LOAD_AHEAD = 4
-STORE_LAG = 2
+LOAD_AHEAD = 6
+STORE_LAG = STEPS - LOAD_AHEAD - 3
 
 FLOPS = 2 * NODES * D * H * 2 * GATES
 

@@ -23,7 +23,8 @@ BANK_GROUPS = 4
 PG = GROUP_NODES // SLOTS
 PB = PG * BANK_GROUPS
 LOAD_AHEAD = 6
-STORE_LAG = STEPS - LOAD_AHEAD - 3
+FC_LATER = 3
+STORE_LAG = STEPS - LOAD_AHEAD - 3 + FC_LATER
 
 FLOPS = 2 * NODES * D * H * 2 * GATES
 
@@ -47,39 +48,58 @@ def tile_childsumtreelstmcell_pb_t_kernel(
             "(b g q) d -> b q g d", g=BANK_GROUPS, q=P
         )
 
-        def load_w(dst, mat):
-            nc.sync.dma_start(
-                out=dst.rearrange("w (u e) c -> w u (e c)", u=2),
-                in_=mat.rearrange("(u w e) c -> w u (e c)", u=2, e=2),
-            )
+        x_sb, fc_sb, ch_sb, hT_ps, xT_ps = {}, {}, {}, {}, {}
+        x_side, h_side, x_q, h_q, io_ps, u_ps = {}, {}, {}, {}, {}, {}
+        pre, tanh_c, out_sb = {}, {}, {}
 
-        def load_u(dst, mat):
-            nc.sync.dma_start(out=dst, in_=mat.rearrange("(t w) c -> w t c", w=P))
+        def live(s):
+            return 0 <= s < STEPS
 
-        def load_weights(mats, k_order, name):
-            raw = const.tile([P, GATES, PACK, H], BF16, name=name + "_raw")
-            for g, mat in enumerate(mats):
-                k_order(raw[:, g], mat)
-            return raw
-
-        def quantise_weights(raw, copy, name):
-            side = const.tile([P, GATES * H * PACK], BF16, align_bytes=64, name=name + "_side")
-            copy(
-                out=side[:].rearrange("w (g c t) -> w g c t", g=GATES, t=PACK),
-                in_=raw[:].rearrange("w g t c -> w g c t"),
-            )
-            codes = const.tile([P, GATES * H], U32, align_bytes=64, name=name + "_codes")
-            scales = const.tile([P, GATES * H], U8, align_bytes=64, name=name + "_scales")
-            for lo, hi in ((0, 2 * H), (2 * H, 3 * H)):
-                nc.vector.quantize_mx(
-                    out=codes[:, lo:hi].bitcast(FP8X4),
-                    scales=scales[:, lo:hi],
-                    in_=side[:, PACK * lo : PACK * hi],
+        def load(s):
+            if not live(s):
+                return
+            for b in range(SLOTS):
+                ch_sb[s, b] = loads.tile(
+                    [P, BANK_GROUPS, D], BF16, tag="ch", bufs=SLOTS * LOAD_AHEAD, name="ch_sb"
                 )
-            return codes, scales
+                nc.sync.dma_start(out=ch_sb[s, b][:], in_=ch_view[SLOTS * s + b])
+            x_sb[s] = loads.tile([P, SLOTS * D], BF16, tag="x", name="x_sb")
+            nc.sync.dma_start(out=x_sb[s][:], in_=x_view[s])
 
-        u_raw = load_weights((Ui, Uo, Uu), load_u, "u")
-        w_raw = load_weights((Wi, Wo, Wu), load_w, "w")
+        def load_fc(s):
+            if not live(s):
+                return
+            fc_sb[s] = loads.tile([P, SLOTS, H], BF16, tag="fc", name="fc_sb")
+            nc.sync.dma_start(out=fc_sb[s][:].rearrange("p j d -> p (j d)"), in_=fc_view[s])
+
+        load(0)
+
+        w_raw = const.tile([P, GATES, PACK, H], BF16)
+        u_raw = const.tile([P, GATES, PACK, H], BF16)
+        for g, (w_mat, u_mat) in enumerate(((Wi, Ui), (Wo, Uo), (Wu, Uu))):
+            nc.sync.dma_start(
+                out=w_raw[:, g].rearrange("w (u e) c -> w u (e c)", u=2),
+                in_=w_mat.rearrange("(u w e) c -> w u (e c)", u=2, e=2),
+            )
+            nc.sync.dma_start(out=u_raw[:, g], in_=u_mat.rearrange("(t w) c -> w t c", w=P))
+        w_side = const.tile([P, GATES, H, PACK], BF16, align_bytes=64)
+        u_side = const.tile([P, GATES, H, PACK], BF16, align_bytes=64)
+        w_codes = const.tile([P, GATES * H], U32, align_bytes=64)
+        u_codes = const.tile([P, GATES * H], U32, align_bytes=64)
+        w_scales = const.tile([P, GATES * H], U8, align_bytes=64)
+        u_scales = const.tile([P, GATES * H], U8, align_bytes=64)
+
+        def quantise_weights():
+            for g in range(GATES):
+                cols = slice(H * g, H * (g + 1))
+                nc.vector.tensor_copy(out=w_side[:, g], in_=w_raw[:, g].rearrange("w t c -> w c t"))
+                nc.scalar.copy(out=u_side[:, g], in_=u_raw[:, g].rearrange("w t c -> w c t"))
+                for side, codes, scales in ((w_side, w_codes, w_scales), (u_side, u_codes, u_scales)):
+                    nc.vector.quantize_mx(
+                        out=codes[:, cols].bitcast(FP8X4),
+                        scales=scales[:, cols],
+                        in_=side[:, g].rearrange("w c t -> w (c t)"),
+                    )
 
         ident = const.tile([P, P], F32)
         make_identity(nc, ident[:])
@@ -104,17 +124,15 @@ def tile_childsumtreelstmcell_pb_t_kernel(
         sel = const.tile([P, SLOTS, PG], BF16)
         nc.vector.tensor_copy(out=sel[:], in_=sel_nat[:].rearrange("q (a j) -> q j a", j=SLOTS))
 
-        w_codes, w_scales = quantise_weights(w_raw, nc.vector.tensor_copy, "w")
-        u_codes, u_scales = quantise_weights(u_raw, nc.scalar.copy, "u")
         bias = const.tile([P, GATES * H], F32)
 
         def build_bias():
-            bias_io_ps = psum.tile([P, 2 * H], F32, tag="io", bufs=3)
+            bias_io_ps = psum.tile([P, 2 * H], F32, tag="io", bufs=2)
             nc.tensor.matmul(
                 out=bias_io_ps[:], lhsT=ones[:], rhs=bias_rows[:, 0 : 2 * H], start=True, stop=True
             )
             nc.vector.tensor_copy(out=bias[:, 0 : 2 * H], in_=bias_io_ps[:])
-            bias_u_ps = psum.tile([P, SLOTS, H], F32, tag="u", bufs=2)
+            bias_u_ps = psum.tile([P, SLOTS, H], F32, tag="u", bufs=1)
             nc.tensor.matmul(
                 out=bias_u_ps[:, 0, :],
                 lhsT=ones[:],
@@ -124,31 +142,11 @@ def tile_childsumtreelstmcell_pb_t_kernel(
             )
             nc.vector.tensor_copy(out=bias[:, 2 * H : 3 * H], in_=bias_u_ps[:, 0, :])
 
-        x_sb, fc_sb, ch_sb, hT_ps, xT_ps = {}, {}, {}, {}, {}
-        x_side, h_side, x_q, h_q, io_ps, u_ps = {}, {}, {}, {}, {}, {}
-        pre, tanh_c, out_sb = {}, {}, {}
-
-        def live(s):
-            return 0 <= s < STEPS
-
-        def load(s):
-            if not live(s):
-                return
-            x_sb[s] = loads.tile([P, SLOTS * D], BF16, tag="x", name="x_sb")
-            nc.sync.dma_start(out=x_sb[s][:], in_=x_view[s])
-            for b in range(SLOTS):
-                ch_sb[s, b] = loads.tile(
-                    [P, BANK_GROUPS, D], BF16, tag="ch", bufs=SLOTS * (LOAD_AHEAD + 1), name="ch_sb"
-                )
-                nc.sync.dma_start(out=ch_sb[s, b][:], in_=ch_view[SLOTS * s + b])
-            fc_sb[s] = loads.tile([P, SLOTS, H], BF16, tag="fc", bufs=LOAD_AHEAD + 3, name="fc_sb")
-            nc.sync.dma_start(out=fc_sb[s][:].rearrange("p j d -> p (j d)"), in_=fc_view[s])
-
         def sum_children(s):
             if not live(s):
                 return
             for b in range(SLOTS):
-                hT_ps[s, b] = psum.tile([P, SLOTS, PACK, PB], F32, tag="hT", bufs=2, name="hT_ps")
+                hT_ps[s, b] = psum.tile([P, SLOTS, PACK, PB], F32, tag="hT", bufs=2 * SLOTS, name="hT_ps")
                 for g in range(BANK_GROUPS):
                     for t in range(PACK):
                         nc.tensor.matmul(
@@ -200,35 +198,38 @@ def tile_childsumtreelstmcell_pb_t_kernel(
         def multiply(s):
             if not live(s):
                 return
-            u_ps[s] = psum.tile([P, SLOTS, H], F32, tag="u", bufs=2, name="u_ps")
             for j in range(SLOTS):
+                io_ps[s, j] = psum.tile([P, 2 * H], F32, tag="io", bufs=2, name="io_ps")
+            u_ps[s] = psum.tile([P, SLOTS, H], F32, tag="u", bufs=1, name="u_ps")
+            groups = [(io_ps[s, j][:], j, slice(0, 2 * H)) for j in range(SLOTS)]
+            groups += [(u_ps[s][:, j, :], j, slice(2 * H, 3 * H)) for j in range(SLOTS)]
+            for acc, j, cols in groups:
                 nodes = slice(P * j, P * (j + 1))
-                io_ps[s, j] = psum.tile([P, 2 * H], F32, tag="io", bufs=3, name="io_ps")
-                for acc, cols in (
-                    (io_ps[s, j][:], slice(0, 2 * H)),
-                    (u_ps[s][:, j, :], slice(2 * H, 3 * H)),
+                for part, (a_q, b_codes, b_scales) in enumerate(
+                    ((x_q[s], w_codes, w_scales), (h_q[s], u_codes, u_scales))
                 ):
-                    for part, (a_q, b_codes, b_scales) in enumerate(
-                        ((x_q[s], w_codes, w_scales), (h_q[s], u_codes, u_scales))
-                    ):
-                        nc.tensor.matmul_mx(
-                            out=acc,
-                            lhsT=a_q[0][:, nodes].bitcast(FP8X4),
-                            lhsT_scale=a_q[1][:, nodes],
-                            rhs=b_codes[:, cols].bitcast(FP8X4),
-                            rhs_scale=b_scales[:, cols],
-                            start=(part == 0),
-                            stop=(part == 1),
-                        )
+                    nc.tensor.matmul_mx(
+                        out=acc,
+                        lhsT=a_q[0][:, nodes].bitcast(FP8X4),
+                        lhsT_scale=a_q[1][:, nodes],
+                        rhs=b_codes[:, cols].bitcast(FP8X4),
+                        rhs_scale=b_scales[:, cols],
+                        start=(part == 0),
+                        stop=(part == 1),
+                    )
 
-        def add_bias(s):
+        def add_bias_io(s, j):
             if not live(s):
                 return
-            pre[s] = work.tile([P, SLOTS, GATES * H], F32, tag="pre", bufs=4, name="pre")
-            for j in range(SLOTS):
-                nc.vector.tensor_tensor(
-                    out=pre[s][:, j, 0 : 2 * H], in0=io_ps[s, j][:], in1=bias[:, 0 : 2 * H], op=ALU.add
-                )
+            if j == 0:
+                pre[s] = work.tile([P, SLOTS, GATES * H], F32, tag="pre", bufs=4, name="pre")
+            nc.vector.tensor_tensor(
+                out=pre[s][:, j, 0 : 2 * H], in0=io_ps[s, j][:], in1=bias[:, 0 : 2 * H], op=ALU.add
+            )
+
+        def add_bias_u(s):
+            if not live(s):
+                return
             nc.vector.tensor_tensor(
                 out=pre[s][:, :, 2 * H : 3 * H],
                 in0=u_ps[s][:],
@@ -239,9 +240,9 @@ def tile_childsumtreelstmcell_pb_t_kernel(
         def activate(s):
             if not live(s):
                 return
-            gates_io, gate_u = pre[s][:, :, 0 : 2 * H], pre[s][:, :, 2 * H : 3 * H]
-            nc.scalar.activation(out=gates_io, in_=gates_io, func=ACT.Sigmoid)
-            nc.scalar.activation(out=gate_u, in_=gate_u, func=ACT.Tanh)
+            for lo, func in ((0, ACT.Sigmoid), (2 * H, ACT.Tanh), (H, ACT.Sigmoid)):
+                gate = pre[s][:, :, lo : lo + H]
+                nc.scalar.activation(out=gate, in_=gate, func=func)
 
         def cell(s):
             if not live(s):
@@ -273,22 +274,26 @@ def tile_childsumtreelstmcell_pb_t_kernel(
 
         def iteration(t):
             load(t + LOAD_AHEAD)
+            load_fc(t + LOAD_AHEAD - FC_LATER)
             store(t - 3 - STORE_LAG)
-            sum_children(t + 1)
-            copy_x(t + 1)
+            multiply(t)
             hidden(t - 3)
+            copy_x(t + 1)
+            add_bias_io(t, 0)
+            round_h(t + 1)
+            quantise(t + 1, h_side, h_q, "h")
             quantise(t + 1, x_side, x_q, "x")
+            add_bias_io(t, 1)
+            add_bias_u(t)
+            sum_children(t + 2)
+            transpose_x(t + 2)
             activate(t - 1)
             cell(t - 1)
-            round_h(t + 1)
-            multiply(t)
-            add_bias(t)
-            quantise(t + 1, h_side, h_q, "h")
             tanh_cell(t - 2)
-            transpose_x(t + 2)
 
-        for t in range(-LOAD_AHEAD, 0):
+        for t in range(1 - LOAD_AHEAD, 0):
             iteration(t)
+        quantise_weights()
         build_bias()
         for t in range(0, STEPS + 3 + STORE_LAG + 1):
             iteration(t)

@@ -16,15 +16,19 @@ PACK = 4
 NODES, CHILDREN, D, H = 4096, 4, 512, 256
 GATES = 3
 
-SLOTS = 2
-STEPS = NODES // (P * SLOTS)
+SLOTS = 4
+PAIR = 2
+HALVES = SLOTS // PAIR
+CHUNKS = NODES // (P * SLOTS)
+STEPS = CHUNKS * HALVES
 GROUP_NODES = P // CHILDREN
 BANK_GROUPS = 4
+STEP_BANKS = SLOTS // HALVES
 PG = GROUP_NODES // SLOTS
 PB = PG * BANK_GROUPS
-LOAD_AHEAD = 6
+LOAD_AHEAD = 7
 FC_LATER = 3
-STORE_LAG = STEPS - LOAD_AHEAD - 3 + FC_LATER
+STORE_LAG = STEPS - 2 * HALVES - LOAD_AHEAD + FC_LATER
 
 FLOPS = 2 * NODES * D * H * 2 * GATES
 
@@ -36,21 +40,20 @@ def tile_childsumtreelstmcell_pb_t_kernel(
     with ExitStack() as ctx:
         ctx.enter_context(tc.manual_schedule())
         const = ctx.enter_context(tc.tile_pool(name="const", bufs=1))
-        loads = ctx.enter_context(tc.tile_pool(name="loads", bufs=LOAD_AHEAD))
+        loads = ctx.enter_context(tc.tile_pool(name="loads", bufs=4))
         sides = ctx.enter_context(tc.tile_pool(name="sides", bufs=2))
         work = ctx.enter_context(tc.tile_pool(name="work", bufs=2))
         psum = ctx.enter_context(tc.psum_pool(name="psum", bufs=1))
 
-        x_view = x.rearrange("(s p j) d -> s p (j d)", p=P, j=SLOTS)
-        fc_view = fc_sum.rearrange("(s p j) d -> s p (j d)", p=P, j=SLOTS)
-        out_view = out.rearrange("o (s p j) d -> s p o (j d)", p=P, j=SLOTS)
+        x_view = x.rearrange("(c p j) d -> c p (j d)", p=P, j=SLOTS)
+        fc_view = fc_sum.rearrange("(c p j) d -> c p (j d)", p=P, j=SLOTS)
+        out_view = out.rearrange("o (c p j) d -> o c p (j d)", p=P, j=SLOTS)
         ch_view = child_h.rearrange("n k d -> (n k) d").rearrange(
             "(b g q) d -> b q g d", g=BANK_GROUPS, q=P
         )
 
-        x_sb, fc_sb, ch_sb, hT_ps, xT_ps = {}, {}, {}, {}, {}
-        x_side, h_side, x_q, h_q, io_ps, u_ps = {}, {}, {}, {}, {}, {}
-        pre, tanh_c, out_sb = {}, {}, {}
+        ch_sb, hT_ps, xT_ps, x_side, x_q, h_q, io_ps, u_ps, pre, tanh_c = {}, {}, {}, {}, {}, {}, {}, {}, {}, {}
+        x_sb, fc_sb, h_side, out_sb = {}, {}, {}, {}
 
         def live(s):
             return 0 <= s < STEPS
@@ -58,19 +61,23 @@ def tile_childsumtreelstmcell_pb_t_kernel(
         def load(s):
             if not live(s):
                 return
-            for b in range(SLOTS):
+            for b in range(STEP_BANKS):
                 ch_sb[s, b] = loads.tile(
-                    [P, BANK_GROUPS, D], BF16, tag="ch", bufs=SLOTS * LOAD_AHEAD, name="ch_sb"
+                    [P, BANK_GROUPS, D], BF16, tag="ch", bufs=STEP_BANKS * (LOAD_AHEAD - 1), name="ch_sb"
                 )
-                nc.sync.dma_start(out=ch_sb[s, b][:], in_=ch_view[SLOTS * s + b])
-            x_sb[s] = loads.tile([P, SLOTS * D], BF16, tag="x", name="x_sb")
-            nc.sync.dma_start(out=x_sb[s][:], in_=x_view[s])
+                nc.sync.dma_start(out=ch_sb[s, b][:], in_=ch_view[STEP_BANKS * s + b])
+            chunk, half = divmod(s, HALVES)
+            if half == 0:
+                x_sb[chunk] = loads.tile([P, SLOTS * D], BF16, tag="x", name="x_sb")
+                nc.sync.dma_start(out=x_sb[chunk][:], in_=x_view[chunk])
 
         def load_fc(s):
             if not live(s):
                 return
-            fc_sb[s] = loads.tile([P, SLOTS, H], BF16, tag="fc", name="fc_sb")
-            nc.sync.dma_start(out=fc_sb[s][:].rearrange("p j d -> p (j d)"), in_=fc_view[s])
+            chunk, half = divmod(s, HALVES)
+            if half == 0:
+                fc_sb[chunk] = loads.tile([P, SLOTS, H], BF16, tag="fc", name="fc_sb")
+                nc.sync.dma_start(out=fc_sb[chunk][:].rearrange("p j d -> p (j d)"), in_=fc_view[chunk])
 
         load(0)
 
@@ -127,12 +134,12 @@ def tile_childsumtreelstmcell_pb_t_kernel(
         bias = const.tile([P, GATES * H], F32)
 
         def build_bias():
-            bias_io_ps = psum.tile([P, 2 * H], F32, tag="io", bufs=2)
+            bias_io_ps = psum.tile([P, 2 * H], F32, tag="io", bufs=PAIR)
             nc.tensor.matmul(
                 out=bias_io_ps[:], lhsT=ones[:], rhs=bias_rows[:, 0 : 2 * H], start=True, stop=True
             )
             nc.vector.tensor_copy(out=bias[:, 0 : 2 * H], in_=bias_io_ps[:])
-            bias_u_ps = psum.tile([P, SLOTS, H], F32, tag="u", bufs=1)
+            bias_u_ps = psum.tile([P, PAIR, H], F32, tag="u", bufs=1)
             nc.tensor.matmul(
                 out=bias_u_ps[:, 0, :],
                 lhsT=ones[:],
@@ -145,8 +152,10 @@ def tile_childsumtreelstmcell_pb_t_kernel(
         def sum_children(s):
             if not live(s):
                 return
-            for b in range(SLOTS):
-                hT_ps[s, b] = psum.tile([P, SLOTS, PACK, PB], F32, tag="hT", bufs=2 * SLOTS, name="hT_ps")
+            for b in range(STEP_BANKS):
+                hT_ps[s, b] = psum.tile(
+                    [P, SLOTS, PACK, PB], F32, tag="hT", bufs=2 * STEP_BANKS, name="hT_ps"
+                )
                 for g in range(BANK_GROUPS):
                     for t in range(PACK):
                         nc.tensor.matmul(
@@ -160,51 +169,64 @@ def tile_childsumtreelstmcell_pb_t_kernel(
         def round_h(s):
             if not live(s):
                 return
-            h_side[s] = sides.tile([P, SLOTS * P * PACK], BF16, align_bytes=64, tag="h_side", name="h_side")
-            view = h_side[s][:].rearrange("w (j p t) -> w j p t", j=SLOTS, t=PACK)
-            for b in range(SLOTS):
+            chunk, half = divmod(s, HALVES)
+            if half == 0:
+                h_side[chunk] = sides.tile(
+                    [P, SLOTS * P * PACK], BF16, align_bytes=64, tag="h_side", name="h_side"
+                )
+            view = h_side[chunk][:].rearrange("w (j p t) -> w j p t", j=SLOTS, t=PACK)
+            for b in range(STEP_BANKS):
+                lo = PB * (STEP_BANKS * half + b)
                 nc.scalar.copy(
-                    out=view[:, :, PB * b : PB * (b + 1), :],
-                    in_=hT_ps[s, b][:].rearrange("w j t p -> w j p t"),
+                    out=view[:, :, lo : lo + PB, :], in_=hT_ps[s, b][:].rearrange("w j t p -> w j p t")
                 )
 
         def transpose_x(s):
             if not live(s):
                 return
-            xT_ps[s] = psum.tile([P, SLOTS, 2, P], F32, tag="xT", bufs=1, name="xT_ps")
-            words = x_sb[s][:].bitcast(F32)
-            for j in range(SLOTS):
+            chunk, half = divmod(s, HALVES)
+            xT_ps[s] = psum.tile([P, PAIR, 2, P], F32, tag="xT", bufs=1, name="xT_ps")
+            words = x_sb[chunk][:].bitcast(F32)
+            for i in range(PAIR):
                 for u in range(2):
-                    first = (D // 2) * j + P * u
-                    nc.tensor.transpose(xT_ps[s][:, j, u, :], words[:, first : first + P], ident[:])
+                    lo = (D // 2) * (PAIR * half + i) + P * u
+                    nc.tensor.transpose(xT_ps[s][:, i, u, :], words[:, lo : lo + P], ident[:])
 
         def copy_x(s):
             if not live(s):
                 return
-            x_side[s] = sides.tile([P, SLOTS * P * PACK], BF16, align_bytes=64, tag="x_side", name="x_side")
+            x_side[s] = sides.tile([P, PAIR * P * PACK], BF16, align_bytes=64, tag="x_side", name="x_side")
             nc.vector.tensor_copy(
-                out=x_side[s][:].bitcast(F32).rearrange("w (j p u) -> w j p u", j=SLOTS, u=2),
-                in_=xT_ps[s][:].rearrange("w j u p -> w j p u"),
+                out=x_side[s][:].bitcast(F32).rearrange("w (i p u) -> w i p u", i=PAIR, u=2),
+                in_=xT_ps[s][:].rearrange("w i u p -> w i p u"),
             )
 
-        def quantise(s, side, quantised, name):
-            if not live(s):
-                return
-            codes = sides.tile([P, SLOTS * P], U32, align_bytes=64, tag=name + "_codes", name=name + "_codes")
-            scales = sides.tile([P, SLOTS * P], U8, align_bytes=64, tag=name + "_scales", name=name + "_scales")
-            nc.vector.quantize_mx(out=codes[:].bitcast(FP8X4), scales=scales[:], in_=side[s][:])
-            quantised[s] = (codes, scales)
+        def quantise(side, name):
+            codes = sides.tile([P, PAIR * P], U32, align_bytes=64, tag=name + "_codes", name=name + "_codes")
+            scales = sides.tile([P, PAIR * P], U8, align_bytes=64, tag=name + "_scales", name=name + "_scales")
+            nc.vector.quantize_mx(out=codes[:].bitcast(FP8X4), scales=scales[:], in_=side)
+            return codes, scales
+
+        def quantise_x(s):
+            if live(s):
+                x_q[s] = quantise(x_side[s][:], "x")
+
+        def quantise_h(s):
+            if live(s):
+                chunk, half = divmod(s, HALVES)
+                width = PAIR * P * PACK
+                h_q[s] = quantise(h_side[chunk][:, width * half : width * (half + 1)], "h")
 
         def multiply(s):
             if not live(s):
                 return
-            for j in range(SLOTS):
-                io_ps[s, j] = psum.tile([P, 2 * H], F32, tag="io", bufs=2, name="io_ps")
-            u_ps[s] = psum.tile([P, SLOTS, H], F32, tag="u", bufs=1, name="u_ps")
-            groups = [(io_ps[s, j][:], j, slice(0, 2 * H)) for j in range(SLOTS)]
-            groups += [(u_ps[s][:, j, :], j, slice(2 * H, 3 * H)) for j in range(SLOTS)]
-            for acc, j, cols in groups:
-                nodes = slice(P * j, P * (j + 1))
+            for i in range(PAIR):
+                io_ps[s, i] = psum.tile([P, 2 * H], F32, tag="io", bufs=PAIR, name="io_ps")
+            u_ps[s] = psum.tile([P, PAIR, H], F32, tag="u", bufs=1, name="u_ps")
+            groups = [(io_ps[s, i][:], i, slice(0, 2 * H)) for i in range(PAIR)]
+            groups += [(u_ps[s][:, i, :], i, slice(2 * H, 3 * H)) for i in range(PAIR)]
+            for acc, i, cols in groups:
+                nodes = slice(P * i, P * (i + 1))
                 for part, (a_q, b_codes, b_scales) in enumerate(
                     ((x_q[s], w_codes, w_scales), (h_q[s], u_codes, u_scales))
                 ):
@@ -218,13 +240,13 @@ def tile_childsumtreelstmcell_pb_t_kernel(
                         stop=(part == 1),
                     )
 
-        def add_bias_io(s, j):
+        def add_bias_io(s, i):
             if not live(s):
                 return
-            if j == 0:
-                pre[s] = work.tile([P, SLOTS, GATES * H], F32, tag="pre", bufs=4, name="pre")
+            if i == 0:
+                pre[s] = work.tile([P, PAIR, GATES * H], F32, tag="pre", bufs=4, name="pre")
             nc.vector.tensor_tensor(
-                out=pre[s][:, j, 0 : 2 * H], in0=io_ps[s, j][:], in1=bias[:, 0 : 2 * H], op=ALU.add
+                out=pre[s][:, i, 0 : 2 * H], in0=io_ps[s, i][:], in1=bias[:, 0 : 2 * H], op=ALU.add
             )
 
         def add_bias_u(s):
@@ -233,7 +255,7 @@ def tile_childsumtreelstmcell_pb_t_kernel(
             nc.vector.tensor_tensor(
                 out=pre[s][:, :, 2 * H : 3 * H],
                 in0=u_ps[s][:],
-                in1=bias[:, 2 * H : 3 * H].unsqueeze(1).to_broadcast([P, SLOTS, H]),
+                in1=bias[:, 2 * H : 3 * H].unsqueeze(1).to_broadcast([P, PAIR, H]),
                 op=ALU.add,
             )
 
@@ -244,48 +266,63 @@ def tile_childsumtreelstmcell_pb_t_kernel(
                 gate = pre[s][:, :, lo : lo + H]
                 nc.scalar.activation(out=gate, in_=gate, func=func)
 
+        def result(s, o):
+            chunk, half = divmod(s, HALVES)
+            return out_sb[chunk][:, o, PAIR * half : PAIR * (half + 1)]
+
         def cell(s):
             if not live(s):
                 return
-            out_sb[s] = work.tile([P, 2, SLOTS, H], F32, tag="out", bufs=STORE_LAG + 4, name="out_sb")
-            c_new = out_sb[s][:, 1]
+            chunk, half = divmod(s, HALVES)
+            if half == 0:
+                out_sb[chunk] = work.tile([P, 2, SLOTS, H], F32, tag="out", bufs=CHUNKS, name="out_sb")
             nc.gpsimd.tensor_tensor(
-                out=c_new, in0=pre[s][:, :, 0:H], in1=pre[s][:, :, 2 * H : 3 * H], op=ALU.mult
+                out=result(s, 1), in0=pre[s][:, :, 0:H], in1=pre[s][:, :, 2 * H : 3 * H], op=ALU.mult
             )
-            nc.gpsimd.tensor_tensor(out=c_new, in0=c_new, in1=fc_sb[s][:], op=ALU.add)
+            nc.gpsimd.tensor_tensor(
+                out=result(s, 1),
+                in0=result(s, 1),
+                in1=fc_sb[chunk][:, PAIR * half : PAIR * (half + 1)],
+                op=ALU.add,
+            )
 
         def tanh_cell(s):
             if not live(s):
                 return
-            tanh_c[s] = work.tile([P, SLOTS, H], F32, tag="tanh_c", name="tanh_c")
-            nc.scalar.activation(out=tanh_c[s][:], in_=out_sb[s][:, 1], func=ACT.Tanh)
+            tanh_c[s] = work.tile([P, PAIR, H], F32, tag="tanh_c", name="tanh_c")
+            nc.scalar.activation(out=tanh_c[s][:], in_=result(s, 1), func=ACT.Tanh)
 
         def hidden(s):
             if not live(s):
                 return
             nc.vector.tensor_tensor(
-                out=out_sb[s][:, 0], in0=pre[s][:, :, H : 2 * H], in1=tanh_c[s][:], op=ALU.mult
+                out=result(s, 0), in0=pre[s][:, :, H : 2 * H], in1=tanh_c[s][:], op=ALU.mult
             )
 
-        def store(s):
+        def store(s, o):
             if not live(s):
                 return
-            nc.sync.dma_start(out=out_view[s], in_=out_sb[s][:].rearrange("p o j d -> p o (j d)"))
+            chunk, half = divmod(s, HALVES)
+            if half == HALVES - 1:
+                nc.sync.dma_start(
+                    out=out_view[o, chunk], in_=out_sb[chunk][:, o].rearrange("p j d -> p (j d)")
+                )
 
         def iteration(t):
             load(t + LOAD_AHEAD)
             load_fc(t + LOAD_AHEAD - FC_LATER)
-            store(t - 3 - STORE_LAG)
+            store(t - 2 - STORE_LAG, 1)
+            store(t - 3 - STORE_LAG, 0)
             multiply(t)
             hidden(t - 3)
             copy_x(t + 1)
             add_bias_io(t, 0)
-            round_h(t + 1)
-            quantise(t + 1, h_side, h_q, "h")
-            quantise(t + 1, x_side, x_q, "x")
+            round_h(t + 2)
+            quantise_h(t + 1)
+            quantise_x(t + 1)
             add_bias_io(t, 1)
             add_bias_u(t)
-            sum_children(t + 2)
+            sum_children(t + 3)
             transpose_x(t + 2)
             activate(t - 1)
             cell(t - 1)

from contextlib import ExitStack

import concourse.mybir as mybir
from concourse.masks import make_identity

F32 = mybir.dt.float32
BF16 = mybir.dt.bfloat16
U32 = mybir.dt.uint32
U8 = mybir.dt.uint8
FP8X4 = mybir.dt.float8_e4m3fn_x4
ACT = mybir.ActivationFunctionType
ALU = mybir.AluOpType

P = 128
PACK = 4
NODES, CHILDREN, D, H = 4096, 4, 512, 256
GATES = 3

SLOTS = 4
PAIR = 2
HALVES = SLOTS // PAIR
CHUNKS = NODES // (P * SLOTS)
STEPS = CHUNKS * HALVES
GROUP_NODES = P // CHILDREN
BANK_GROUPS = 4
STEP_BANKS = SLOTS // HALVES
PG = GROUP_NODES // SLOTS
PB = PG * BANK_GROUPS
LOAD_AHEAD = 7
FC_LATER = 3
STORE_LAG = STEPS - 2 * HALVES - LOAD_AHEAD + FC_LATER

FLOPS = 2 * NODES * D * H * 2 * GATES


def tile_childsumtreelstmcell_pb_t_kernel(
    tc, x, child_h, fc_sum, Wi, bWi, Ui, bUi, Wo, bWo, Uo, bUo, Wu, bWu, Uu, bUu, out
):
    nc = tc.nc
    with ExitStack() as ctx:
        ctx.enter_context(tc.manual_schedule())
        const = ctx.enter_context(tc.tile_pool(name="const", bufs=1))
        loads = ctx.enter_context(tc.tile_pool(name="loads", bufs=4))
        sides = ctx.enter_context(tc.tile_pool(name="sides", bufs=2))
        work = ctx.enter_context(tc.tile_pool(name="work", bufs=2))
        psum = ctx.enter_context(tc.psum_pool(name="psum", bufs=1))

        x_view = x.rearrange("(c p j) d -> c p (j d)", p=P, j=SLOTS)
        fc_view = fc_sum.rearrange("(c p j) d -> c p (j d)", p=P, j=SLOTS)
        out_view = out.rearrange("o (c p j) d -> o c p (j d)", p=P, j=SLOTS)
        ch_view = child_h.rearrange("n k d -> (n k) d").rearrange(
            "(b g q) d -> b q g d", g=BANK_GROUPS, q=P
        )

        ch_sb, hT_ps, xT_ps, x_side, x_q, h_q, io_ps, u_ps, pre, tanh_c = {}, {}, {}, {}, {}, {}, {}, {}, {}, {}
        x_sb, fc_sb, h_side, out_sb = {}, {}, {}, {}

        def live(s):
            return 0 <= s < STEPS

        def load(s):
            if not live(s):
                return
            for b in range(STEP_BANKS):
                ch_sb[s, b] = loads.tile(
                    [P, BANK_GROUPS, D], BF16, tag="ch", bufs=STEP_BANKS * (LOAD_AHEAD - 1), name="ch_sb"
                )
                nc.sync.dma_start(out=ch_sb[s, b][:], in_=ch_view[STEP_BANKS * s + b])
            chunk, half = divmod(s, HALVES)
            if half == 0:
                x_sb[chunk] = loads.tile([P, SLOTS * D], BF16, tag="x", name="x_sb")
                nc.sync.dma_start(out=x_sb[chunk][:], in_=x_view[chunk])

        def load_fc(s):
            if not live(s):
                return
            chunk, half = divmod(s, HALVES)
            if half == 0:
                fc_sb[chunk] = loads.tile([P, SLOTS, H], BF16, tag="fc", name="fc_sb")
                nc.sync.dma_start(out=fc_sb[chunk][:].rearrange("p j d -> p (j d)"), in_=fc_view[chunk])

        load(0)

        w_raw = const.tile([P, GATES, PACK, H], BF16)
        u_raw = const.tile([P, GATES, PACK, H], BF16)
        for g, (w_mat, u_mat) in enumerate(((Wi, Ui), (Wo, Uo), (Wu, Uu))):
            nc.sync.dma_start(
                out=w_raw[:, g].rearrange("w (u e) c -> w u (e c)", u=2),
                in_=w_mat.rearrange("(u w e) c -> w u (e c)", u=2, e=2),
            )
            nc.sync.dma_start(out=u_raw[:, g], in_=u_mat.rearrange("(t w) c -> w t c", w=P))
        w_side = const.tile([P, GATES, H, PACK], BF16, align_bytes=64)
        u_side = const.tile([P, GATES, H, PACK], BF16, align_bytes=64)
        w_codes = const.tile([P, GATES * H], U32, align_bytes=64)
        u_codes = const.tile([P, GATES * H], U32, align_bytes=64)
        w_scales = const.tile([P, GATES * H], U8, align_bytes=64)
        u_scales = const.tile([P, GATES * H], U8, align_bytes=64)

        def quantise_weights():
            for g in range(GATES):
                cols = slice(H * g, H * (g + 1))
                nc.vector.tensor_copy(out=w_side[:, g], in_=w_raw[:, g].rearrange("w t c -> w c t"))
                nc.scalar.copy(out=u_side[:, g], in_=u_raw[:, g].rearrange("w t c -> w c t"))
                for side, codes, scales in ((w_side, w_codes, w_scales), (u_side, u_codes, u_scales)):
                    nc.vector.quantize_mx(
                        out=codes[:, cols].bitcast(FP8X4),
                        scales=scales[:, cols],
                        in_=side[:, g].rearrange("w c t -> w (c t)"),
                    )

        ident = const.tile([P, P], F32)
        make_identity(nc, ident[:])
        bias_rows = const.tile([P, GATES * H], BF16)
        nc.vector.memset(bias_rows[:], 0.0)
        for g, (b_w, b_u) in enumerate(((bWi, bUi), (bWo, bUo), (bWu, bUu))):
            cols = slice(H * g, H * (g + 1))
            nc.gpsimd.dma_start(out=bias_rows[0:1, cols], in_=b_w.rearrange("(o h) -> o h", o=1))
            nc.gpsimd.dma_start(out=bias_rows[1:2, cols], in_=b_u.rearrange("(o h) -> o h", o=1))
        ones = const.tile([P, P], BF16)
        nc.vector.memset(ones[:], 1.0)
        warm = const.tile([P, 1], F32)
        nc.vector.memset(warm[:], 0.0)
        nc.scalar.activation(out=warm[:], in_=warm[:], func=ACT.Sigmoid)
        sel_nat = const.tile([P, GROUP_NODES], F32)
        nc.vector.tensor_reduce(
            out=sel_nat[:],
            in_=ident[:].rearrange("q (n k) -> q n k", k=CHILDREN),
            axis=mybir.AxisListType.X,
            op=ALU.add,
        )
        sel = const.tile([P, SLOTS, PG], BF16)
        nc.vector.tensor_copy(out=sel[:], in_=sel_nat[:].rearrange("q (a j) -> q j a", j=SLOTS))

        bias = const.tile([P, GATES * H], F32)

        def build_bias():
            bias_io_ps = psum.tile([P, 2 * H], F32, tag="io", bufs=PAIR)
            nc.tensor.matmul(
                out=bias_io_ps[:], lhsT=ones[:], rhs=bias_rows[:, 0 : 2 * H], start=True, stop=True
            )
            nc.vector.tensor_copy(out=bias[:, 0 : 2 * H], in_=bias_io_ps[:])
            bias_u_ps = psum.tile([P, PAIR, H], F32, tag="u", bufs=1)
            nc.tensor.matmul(
                out=bias_u_ps[:, 0, :],
                lhsT=ones[:],
                rhs=bias_rows[:, 2 * H : 3 * H],
                start=True,
                stop=True,
            )
            nc.vector.tensor_copy(out=bias[:, 2 * H : 3 * H], in_=bias_u_ps[:, 0, :])

        def sum_children(s):
            if not live(s):
                return
            for b in range(STEP_BANKS):
                hT_ps[s, b] = psum.tile(
                    [P, SLOTS, PACK, PB], F32, tag="hT", bufs=2 * STEP_BANKS, name="hT_ps"
                )
                for g in range(BANK_GROUPS):
                    for t in range(PACK):
                        nc.tensor.matmul(
                            out=hT_ps[s, b][:, :, t, PG * g : PG * (g + 1)],
                            lhsT=ch_sb[s, b][:, g, P * t : P * (t + 1)],
                            rhs=sel[:],
                            start=True,
                            stop=True,
                        )

        def round_h(s):
            if not live(s):
                return
            chunk, half = divmod(s, HALVES)
            if half == 0:
                h_side[chunk] = sides.tile(
                    [P, SLOTS * P * PACK], BF16, align_bytes=64, tag="h_side", name="h_side"
                )
            view = h_side[chunk][:].rearrange("w (j p t) -> w j p t", j=SLOTS, t=PACK)
            for b in range(STEP_BANKS):
                lo = PB * (STEP_BANKS * half + b)
                nc.scalar.copy(
                    out=view[:, :, lo : lo + PB, :], in_=hT_ps[s, b][:].rearrange("w j t p -> w j p t")
                )

        def transpose_x(s):
            if not live(s):
                return
            chunk, half = divmod(s, HALVES)
            xT_ps[s] = psum.tile([P, PAIR, 2, P], F32, tag="xT", bufs=1, name="xT_ps")
            words = x_sb[chunk][:].bitcast(F32)
            for i in range(PAIR):
                for u in range(2):
                    lo = (D // 2) * (PAIR * half + i) + P * u
                    nc.tensor.transpose(xT_ps[s][:, i, u, :], words[:, lo : lo + P], ident[:])

        def copy_x(s):
            if not live(s):
                return
            x_side[s] = sides.tile([P, PAIR * P * PACK], BF16, align_bytes=64, tag="x_side", name="x_side")
            nc.vector.tensor_copy(
                out=x_side[s][:].bitcast(F32).rearrange("w (i p u) -> w i p u", i=PAIR, u=2),
                in_=xT_ps[s][:].rearrange("w i u p -> w i p u"),
            )

        def quantise(side, name):
            codes = sides.tile([P, PAIR * P], U32, align_bytes=64, tag=name + "_codes", name=name + "_codes")
            scales = sides.tile([P, PAIR * P], U8, align_bytes=64, tag=name + "_scales", name=name + "_scales")
            nc.vector.quantize_mx(out=codes[:].bitcast(FP8X4), scales=scales[:], in_=side)
            return codes, scales

        def quantise_x(s):
            if live(s):
                x_q[s] = quantise(x_side[s][:], "x")

        def quantise_h(s):
            if live(s):
                chunk, half = divmod(s, HALVES)
                width = PAIR * P * PACK
                h_q[s] = quantise(h_side[chunk][:, width * half : width * (half + 1)], "h")

        def multiply(s):
            if not live(s):
                return
            for i in range(PAIR):
                io_ps[s, i] = psum.tile([P, 2 * H], F32, tag="io", bufs=PAIR, name="io_ps")
            u_ps[s] = psum.tile([P, PAIR, H], F32, tag="u", bufs=1, name="u_ps")
            groups = [(io_ps[s, i][:], i, slice(0, 2 * H)) for i in range(PAIR)]
            groups += [(u_ps[s][:, i, :], i, slice(2 * H, 3 * H)) for i in range(PAIR)]
            for acc, i, cols in groups:
                nodes = slice(P * i, P * (i + 1))
                for part, (a_q, b_codes, b_scales) in enumerate(
                    ((x_q[s], w_codes, w_scales), (h_q[s], u_codes, u_scales))
                ):
                    nc.tensor.matmul_mx(
                        out=acc,
                        lhsT=a_q[0][:, nodes].bitcast(FP8X4),
                        lhsT_scale=a_q[1][:, nodes],
                        rhs=b_codes[:, cols].bitcast(FP8X4),
                        rhs_scale=b_scales[:, cols],
                        start=(part == 0),
                        stop=(part == 1),
                    )

        def add_bias_io(s, i):
            if not live(s):
                return
            if i == 0:
                pre[s] = work.tile([P, PAIR, GATES * H], F32, tag="pre", bufs=4, name="pre")
            nc.vector.tensor_tensor(
                out=pre[s][:, i, 0 : 2 * H], in0=io_ps[s, i][:], in1=bias[:, 0 : 2 * H], op=ALU.add
            )

        def add_bias_u(s):
            if not live(s):
                return
            nc.vector.tensor_tensor(
                out=pre[s][:, :, 2 * H : 3 * H],
                in0=u_ps[s][:],
                in1=bias[:, 2 * H : 3 * H].unsqueeze(1).to_broadcast([P, PAIR, H]),
                op=ALU.add,
            )

        def activate(s):
            if not live(s):
                return
            for lo, func in ((0, ACT.Sigmoid), (2 * H, ACT.Tanh), (H, ACT.Sigmoid)):
                gate = pre[s][:, :, lo : lo + H]
                nc.scalar.activation(out=gate, in_=gate, func=func)

        def result(s, o):
            chunk, half = divmod(s, HALVES)
            return out_sb[chunk][:, o, PAIR * half : PAIR * (half + 1)]

        def cell(s):
            if not live(s):
                return
            chunk, half = divmod(s, HALVES)
            if half == 0:
                out_sb[chunk] = work.tile([P, 2, SLOTS, H], F32, tag="out", bufs=CHUNKS, name="out_sb")
            nc.gpsimd.tensor_tensor(
                out=result(s, 1), in0=pre[s][:, :, 0:H], in1=pre[s][:, :, 2 * H : 3 * H], op=ALU.mult
            )
            nc.gpsimd.tensor_tensor(
                out=result(s, 1),
                in0=result(s, 1),
                in1=fc_sb[chunk][:, PAIR * half : PAIR * (half + 1)],
                op=ALU.add,
            )

        def tanh_cell(s):
            if not live(s):
                return
            tanh_c[s] = work.tile([P, PAIR, H], F32, tag="tanh_c", name="tanh_c")
            nc.scalar.activation(out=tanh_c[s][:], in_=result(s, 1), func=ACT.Tanh)

        def hidden(s):
            if not live(s):
                return
            nc.vector.tensor_tensor(
                out=result(s, 0), in0=pre[s][:, :, H : 2 * H], in1=tanh_c[s][:], op=ALU.mult
            )

        def store(s, o):
            if not live(s):
                return
            chunk, half = divmod(s, HALVES)
            if half == HALVES - 1:
                nc.sync.dma_start(
                    out=out_view[o, chunk], in_=out_sb[chunk][:, o].rearrange("p j d -> p (j d)")
                )

        def iteration(t):
            load(t + LOAD_AHEAD)
            load_fc(t + LOAD_AHEAD - FC_LATER)
            store(t - 2 - STORE_LAG, 1)
            store(t - 3 - STORE_LAG, 0)
            multiply(t)
            hidden(t - 3)
            copy_x(t + 1)
            add_bias_io(t, 0)
            round_h(t + 2)
            quantise_h(t + 1)
            quantise_x(t + 1)
            add_bias_io(t, 1)
            add_bias_u(t)
            sum_children(t + 3)
            transpose_x(t + 2)
            activate(t - 1)
            cell(t - 1)
            tanh_cell(t - 2)

        for t in range(1 - LOAD_AHEAD, 0):
            iteration(t)
        quantise_weights()
        build_bias()
        for t in range(0, STEPS + 3 + STORE_LAG + 1):
            iteration(t)
